import numpy as np
import ml_dtypes


def mxq(x, axis, fmt="e4m3"):
    dtype, down = {"e4m3": (ml_dtypes.float8_e4m3fn, 7), "e5m2": (ml_dtypes.float8_e5m2, 14)}[fmt]
    v = np.moveaxis(np.asarray(x, np.float32).astype(ml_dtypes.bfloat16).astype(np.float64), axis, -1)
    blocks = v.reshape(v.shape[:-1] + (-1, 32))
    amax = np.abs(blocks).max(-1, keepdims=True)
    byte = np.maximum(np.where(amax > 0, np.frexp(amax)[1] - 1 + 127, 0) - down, 1)
    scale = np.exp2(byte - 127.0)
    codes = (blocks / scale).astype(np.float32).astype(dtype).astype(np.float64)
    return np.moveaxis((codes * scale).reshape(v.shape), -1, axis)


WIDE = False


def mx_kscale(k):
    if not WIDE:
        return np.ones(k)
    levels = np.array([10, -10, 5, -5, 0])
    a = np.random.permutation(np.resize(levels, k // 512 * 4)).reshape(k // 512, 4)
    idx = np.arange(k)
    return np.exp2(a[idx // 512, idx % 128 // 32])


BF16 = ml_dtypes.bfloat16


def bf(x):
    return np.asarray(x, np.float32).astype(BF16)


def f64(x):
    return np.asarray(x).astype(np.float64)


NB, DI, DO, B = 8, 1024, 1024, 256
F = NB * DO
EPS = 1e-5


def setup_inputs():
    s, t = mx_kscale(DI), mx_kscale(F)
    tk = t.reshape(NB, DO)
    return {"x": bf(np.random.standard_normal((B, DI)) * s),
            "W": bf(np.random.standard_normal((NB, DI, DO)) / np.sqrt(DI) / s[None, :, None]),
            "b": bf(np.random.standard_normal((NB, DO)) * 0.5),
            "gamma": bf((1.0 + 0.2 * np.random.standard_normal((NB, DO))) * tk),
            "beta": bf(0.2 * np.random.standard_normal((NB, DO)) * tk),
            "Wf1": bf(np.random.standard_normal((F, DO)) / np.sqrt(F) / t[:, None]),
            "bf1": bf(np.random.standard_normal(DO) * 0.3)}


def reference(x, W, b, gamma, beta, Wf1, bf1):
    w2 = f64(W).transpose(1, 0, 2).reshape(DI, F)
    h = (mxq(f64(x), 1, "e4m3") @ mxq(w2, 0, "e4m3")).reshape(B, NB, DO) + f64(b)[None]
    h = np.maximum(h, 0.0)
    mean = h.mean(axis=0, keepdims=True)
    var = ((h - mean) ** 2).mean(axis=0, keepdims=True)
    h = (h - mean) * (1.0 / np.sqrt(var + EPS)) * f64(gamma)[None] + f64(beta)[None]
    fused = h.reshape(B, F)
    return np.maximum((mxq(fused, 1, "e4m3") @ mxq(f64(Wf1), 0, "e4m3")) + f64(bf1), 0.0)

@@ -1,0 +1,319 @@
+from contextlib import ExitStack
+
+import concourse.mybir as mybir
+from concourse.masks import make_identity
+
+F32 = mybir.dt.float32
+BF16 = mybir.dt.bfloat16
+U32 = mybir.dt.uint32
+U8 = mybir.dt.uint8
+FP8X4 = mybir.dt.float8_e4m3fn_x4
+ACT = mybir.ActivationFunctionType
+ALU = mybir.AluOpType
+
+P = 128
+PACK = 4
+K_PASS = P * PACK
+NB, DI, DO, B = 8, 1024, 1024, 256
+F = NB * DO
+EPS = 1e-5
+FLOPS = 2 * B * DI * F + 2 * B * F * DO
+
+TILES = DO // P
+GROUPS = DO // K_PASS
+W_PASSES = DI // K_PASS
+W_SLABS = NB * W_PASSES
+SLABS = W_SLABS + F // K_PASS
+ROUND_SLABS = 2
+ROUNDS = SLABS // ROUND_SLABS
+N_TILE = 512
+RUN = 4
+
+RAW_BUFS = 10
+VECTOR_COLS_BN = 640
+VECTOR_COLS = 512
+
+
+def tile_extremeoptimizationlayer_pa_kernel(tc, x, W, b, gamma, beta, Wf1, bf1, out):
+    nc = tc.nc
+    with ExitStack() as ctx:
+        ctx.enter_context(tc.manual_schedule())
+        const = ctx.enter_context(tc.tile_pool(name="const", bufs=1))
+        raw_pool = ctx.enter_context(tc.tile_pool(name="raw", bufs=RAW_BUFS))
+        slab_pool = ctx.enter_context(tc.tile_pool(name="slab", bufs=2 * ROUND_SLABS))
+        branch_pool = ctx.enter_context(tc.tile_pool(name="branch", bufs=2))
+        result_pool = ctx.enter_context(tc.tile_pool(name="result", bufs=4))
+        psum_h = ctx.enter_context(tc.psum_pool(name="psum_h", bufs=4))
+        psum_acc = ctx.enter_context(tc.psum_pool(name="psum_acc", bufs=1))
+
+        raw_of = {}
+        grouped_of = {}
+        codes_of = {}
+        h_of = {}
+        bn = {}
+
+        def load_slab(s):
+            if s >= SLABS:
+                return
+            raw = raw_pool.tile([P, PACK, DO], BF16, name="raw")
+            if s < W_SLABS:
+                rows = W[s // W_PASSES, (s % W_PASSES) * K_PASS : (s % W_PASSES + 1) * K_PASS, :]
+                nc.sync.dma_start(out=raw[:], in_=rows.rearrange("(p t) w -> p t w", t=PACK))
+            else:
+                g = s - W_SLABS
+                rows = Wf1[g * K_PASS : (g + 1) * K_PASS, :]
+                nc.sync.dma_start(out=raw[:], in_=rows.rearrange("(t p) w -> p t w", p=P))
+            raw_of[s] = raw
+
+        def regroup_slab(s, vector_cols):
+            if s >= SLABS:
+                return
+            grouped = slab_pool.tile([P, DO, PACK], BF16, name="grouped", align_bytes=64)
+            src = raw_of[s].rearrange("p t (c i) -> p c t i", i=RUN)
+            dst = grouped.rearrange("p (c i) t -> p c t i", i=RUN)
+            cut = vector_cols // RUN
+            nc.vector.tensor_copy(out=dst[:, :cut], in_=src[:, :cut])
+            nc.scalar.copy(out=dst[:, cut:], in_=src[:, cut:])
+            grouped_of[s] = grouped
+
+        def quantise_slab(s):
+            if s < 0:
+                return
+            codes = slab_pool.tile([P, DO], U32, name="codes", align_bytes=64)
+            scales = slab_pool.tile([P, DO], U8, name="scales", align_bytes=64)
+            nc.vector.quantize_mx(
+                out=codes[:].bitcast(FP8X4),
+                scales=scales[:],
+                in_=grouped_of[s].rearrange("p w t -> p (w t)"),
+            )
+            codes_of[s] = (codes, scales)
+
+        def stage1(br):
+            h_of[br] = []
+            for pair in range(TILES // 2):
+                h = psum_h.tile([P, 2, B], F32, name="h")
+                for half in range(2):
+                    cols = slice((2 * pair + half) * P, (2 * pair + half + 1) * P)
+                    for c in range(W_PASSES):
+                        codes, scales = codes_of[W_PASSES * br + c]
+                        nc.tensor.matmul_mx(
+                            out=h[:, half, :],
+                            lhsT=codes[:, cols].bitcast(FP8X4),
+                            lhsT_scale=scales[:, cols],
+                            rhs=x_codes[:, c * B : (c + 1) * B].bitcast(FP8X4),
+                            rhs_scale=x_scales[:, c * B : (c + 1) * B],
+                            start=(c == 0),
+                            stop=(c == W_PASSES - 1),
+                        )
+                h_of[br].append(h)
+
+        def stage2(g):
+            codes, scales = codes_of[W_SLABS + g]
+            for bt in range(B // P):
+                rows = slice(bt * P, (bt + 1) * P)
+                for nt in range(DO // N_TILE):
+                    cols = slice(nt * N_TILE, (nt + 1) * N_TILE)
+                    nc.tensor.matmul_mx(
+                        out=acc[bt][nt][:],
+                        lhsT=f_codes[:, g, rows].bitcast(FP8X4),
+                        lhsT_scale=f_scales[:, g, rows],
+                        rhs=codes[:, cols].bitcast(FP8X4),
+                        rhs_scale=scales[:, cols],
+                        start=(g == 0),
+                        stop=(g == F // K_PASS - 1),
+                    )
+
+        def live(br):
+            return 0 <= br < NB
+
+        def stat_tile(name, br):
+            bn[(name, br)] = branch_pool.tile([P, TILES], F32, name=name)
+            return bn[(name, br)]
+
+        def relu_and_sums(br):
+            if not live(br):
+                return
+            a = branch_pool.tile([P, TILES, B], F32, name="a")
+            bn[("a", br)] = a
+            sums = stat_tile("sums", br)
+            for i in range(TILES):
+                nc.scalar.activation(
+                    out=a[:, i, :],
+                    in_=h_of[br][i // 2][:, i % 2, :],
+                    func=ACT.Relu,
+                    bias=b_col[:, TILES * br + i : TILES * br + i + 1],
+                    accum_out=sums[:, i : i + 1],
+                )
+
+        def negative_mean(br):
+            if live(br):
+                nc.scalar.mul(out=stat_tile("neg_mean", br)[:], in_=bn[("sums", br)][:], mul=-1.0 / B)
+
+        def squares(br):
+            if not live(br):
+                return
+            unused = branch_pool.tile([P, TILES, B], BF16, name="unused")
+            sumsq = stat_tile("sumsq", br)
+            for i in range(TILES):
+                nc.scalar.activation(
+                    out=unused[:, i, :],
+                    in_=bn[("a", br)][:, i, :],
+                    func=ACT.Square,
+                    bias=bn[("neg_mean", br)][:, i : i + 1],
+                    accum_out=sumsq[:, i : i + 1],
+                )
+
+        def standard_deviation(br):
+            if live(br):
+                nc.scalar.activation(
+                    out=stat_tile("std", br)[:], in_=bn[("sumsq", br)][:], func=ACT.Sqrt, bias=eps_col[:], scale=1.0 / B
+                )
+
+        def reciprocal_std(br):
+            if live(br):
+                nc.vector.reciprocal(out=stat_tile("rstd", br)[:], in_=bn[("std", br)][:])
+
+        def gain(br):
+            if live(br):
+                nc.vector.tensor_mul(
+                    out=stat_tile("gain", br)[:], in0=bn[("rstd", br)][:], in1=gamma_col[:, TILES * br : TILES * (br + 1)]
+                )
+
+        def negative_mean_times_gain(br):
+            if live(br):
+                nc.vector.tensor_mul(out=stat_tile("moved", br)[:], in0=bn[("neg_mean", br)][:], in1=bn[("gain", br)][:])
+
+        def shift(br):
+            if live(br):
+                nc.vector.tensor_add(
+                    out=stat_tile("shift", br)[:], in0=bn[("moved", br)][:], in1=beta_col[:, TILES * br : TILES * (br + 1)]
+                )
+
+        def normalise(br):
+            if not live(br):
+                return
+            normed = branch_pool.tile([P, TILES, B], BF16, name="normed")
+            bn[("normed", br)] = normed
+            for i in range(TILES):
+                nc.vector.tensor_scalar(
+                    out=normed[:, i, :],
+                    in0=bn[("a", br)][:, i, :],
+                    scalar1=bn[("gain", br)][:, i : i + 1],
+                    scalar2=bn[("shift", br)][:, i : i + 1],
+                    op0=ALU.mult,
+                    op1=ALU.add,
+                )
+
+        def regroup_fused(br, j):
+            if not live(br):
+                return
+            if j == 0:
+                bn[("f_grouped", br)] = branch_pool.tile([P, GROUPS, B, PACK], BF16, name="f_grouped", align_bytes=64)
+            nc.vector.tensor_copy(
+                out=bn[("f_grouped", br)][:, j].rearrange("p (c i) t -> p c t i", i=RUN),
+                in_=bn[("normed", br)][:, PACK * j : PACK * (j + 1), :].rearrange("p t (c i) -> p c t i", i=RUN),
+            )
+
+        def quantise_fused(br):
+            if live(br):
+                passes = slice(GROUPS * br, GROUPS * (br + 1))
+                nc.vector.quantize_mx(
+                    out=f_codes[:, passes, :].rearrange("p g n -> p (g n)").bitcast(FP8X4),
+                    scales=f_scales[:, passes, :].rearrange("p g n -> p (g n)"),
+                    in_=bn[("f_grouped", br)].rearrange("p g n t -> p (g n t)"),
+                )
+
+        x_sb = const.tile([P, (B // P) * DI], BF16, name="x_sb")
+        nc.sync.dma_start(
+            out=x_sb.rearrange("p (bt k) -> p bt k", k=DI), in_=x.rearrange("(bt p) k -> p bt k", p=P)
+        )
+        for s in range(RAW_BUFS):
+            load_slab(s)
+        bias_all = const.tile([P, DO], BF16, name="bias_all")
+        nc.sync.dma_start(out=bias_all[:], in_=bf1.partition_broadcast(P))
+
+        rows_b_gamma = const.tile([P, P], BF16, name="rows_b_gamma")
+        rows_beta = const.tile([P, P], BF16, name="rows_beta")
+        nc.vector.memset(rows_beta[:], 0.0)
+        eps_col = const.tile([P, 1], F32, name="eps_col")
+        nc.vector.memset(eps_col[:], EPS)
+        param_rows = NB * TILES
+        nc.scalar.dma_start(out=rows_b_gamma[:param_rows, :], in_=b.rearrange("k (i p) -> (k i) p", p=P))
+        nc.scalar.dma_start(out=rows_b_gamma[param_rows:, :], in_=gamma.rearrange("k (i p) -> (k i) p", p=P))
+        nc.scalar.dma_start(out=rows_beta[:param_rows, :], in_=beta.rearrange("k (i p) -> (k i) p", p=P))
+        first_sqrt = const.tile([P, 1], F32, name="first_sqrt")
+        nc.scalar.activation(out=first_sqrt[:], in_=eps_col[:], func=ACT.Sqrt)
+
+        ident_f32 = const.tile([P, P], F32, name="ident_f32")
+        make_identity(nc, ident_f32[:])
+        ident_bf16 = const.tile([P, P], BF16, name="ident_bf16")
+        make_identity(nc, ident_bf16[:])
+
+        x_words = x_sb[:].bitcast(F32).rearrange("p (bt c q u) -> p bt c q u", bt=B // P, c=W_PASSES, q=P)
+        x_grouped = const.tile([P, W_PASSES * B * PACK], BF16, name="x_grouped", align_bytes=64)
+        x_grouped_words = x_grouped[:].bitcast(F32).rearrange("p (c n u) -> p c n u", c=W_PASSES, n=B)
+        x_t = []
+        for c in range(W_PASSES):
+            x_t.append(psum_h.tile([P, 2, B], F32, name="h"))
+            for u in range(2):
+                for bt in range(B // P):
+                    nc.tensor.transpose(x_t[c][:, u, bt * P : (bt + 1) * P], x_words[:, bt, c, :, u], ident_f32[:])
+        params_t = psum_h.tile([P, 2, P], BF16, name="h")
+        nc.tensor.transpose(params_t[:, 0, :], rows_b_gamma[:], ident_bf16[:])
+        nc.tensor.transpose(params_t[:, 1, :], rows_beta[:], ident_bf16[:])
+        nc.vector.tensor_copy(out=x_grouped_words[:, 0], in_=x_t[0].rearrange("p u n -> p n u"))
+        nc.scalar.copy(out=x_grouped_words[:, 1], in_=x_t[1].rearrange("p u n -> p n u"))
+        params = const.tile([P, 2, P], F32, name="params")
+        nc.vector.tensor_copy(out=params[:], in_=params_t[:])
+        b_col = params[:, 0, :param_rows]
+        gamma_col = params[:, 0, param_rows:]
+        beta_col = params[:, 1, :param_rows]
+        x_codes = const.tile([P, W_PASSES * B], U32, name="x_codes", align_bytes=64)
+        x_scales = const.tile([P, W_PASSES * B], U8, name="x_scales", align_bytes=64)
+        nc.vector.quantize_mx(out=x_codes[:].bitcast(FP8X4), scales=x_scales[:], in_=x_grouped[:])
+
+        f_codes = const.tile([P, F // K_PASS, B], U32, name="f_codes", align_bytes=64)
+        f_scales = const.tile([P, F // K_PASS, B], U8, name="f_scales", align_bytes=64)
+        acc = [
+            [psum_acc.tile([P, N_TILE], F32, name="acc%d%d" % (bt, nt)) for nt in range(DO // N_TILE)]
+            for bt in range(B // P)
+        ]
+
+        for r in range(ROUNDS + 1):
+            scalar_has_bn = live(r - 2)
+            vector_cols = VECTOR_COLS_BN if scalar_has_bn else VECTOR_COLS
+            first = ROUND_SLABS * r
+
+            relu_and_sums(r - 2)
+            standard_deviation(r - 3)
+            quantise_slab(first - 2)
+            quantise_slab(first - 1)
+            if 1 <= r <= NB:
+                stage1(r - 1)
+            if r > NB:
+                stage2(first - 2 - W_SLABS)
+                stage2(first - 1 - W_SLABS)
+
+            regroup_slab(first, vector_cols)
+            reciprocal_std(r - 3)
+            negative_mean(r - 2)
+            regroup_slab(first + 1, vector_cols)
+            load_slab(first + RAW_BUFS)
+            load_slab(first + RAW_BUFS + 1)
+            squares(r - 2)
+
+            gain(r - 3)
+            regroup_fused(r - 4, 0)
+            negative_mean_times_gain(r - 3)
+            regroup_fused(r - 4, 1)
+            shift(r - 3)
+            normalise(r - 3)
+            quantise_fused(r - 4)
+
+        for bt in range(B // P):
+            for nt in range(DO // N_TILE):
+                cols = slice(nt * N_TILE, (nt + 1) * N_TILE)
+                result = result_pool.tile([P, N_TILE], F32, name="result")
+                nc.vector.tensor_tensor(out=result[:], in0=acc[bt][nt][:], in1=bias_all[:, cols], op=ALU.add)
+                nc.scalar.activation(out=result[:], in_=result[:], func=ACT.Relu)
+                nc.sync.dma_start(out=out[bt * P : (bt + 1) * P, cols], in_=result[:])

@@ -30,8 +30,10 @@ N_TILE = 512
 RUN = 4
 
 RAW_BUFS = 10
-VECTOR_COLS_BN = 640
-VECTOR_COLS = 512
+BASE_COLS = 512
+RELU_SQUARES_COLS = 416
+NORMALISE_COLS = 128
+FUSED_COLS = 128
 
 
 def tile_extremeoptimizationlayer_pa_kernel(tc, x, W, b, gamma, beta, Wf1, bf1, out):
@@ -224,20 +226,22 @@ def tile_extremeoptimizationlayer_pa_kernel(tc, x, W, b, gamma, beta, Wf1, bf1, 
                 )
 
         x_sb = const.tile([P, (B // P) * DI], BF16, name="x_sb")
+        for s in range(ROUND_SLABS):
+            load_slab(s)
         nc.sync.dma_start(
             out=x_sb.rearrange("p (bt k) -> p bt k", k=DI), in_=x.rearrange("(bt p) k -> p bt k", p=P)
         )
-        for s in range(RAW_BUFS):
+        for s in range(ROUND_SLABS, RAW_BUFS):
             load_slab(s)
         bias_all = const.tile([P, DO], BF16, name="bias_all")
         nc.sync.dma_start(out=bias_all[:], in_=bf1.partition_broadcast(P))
 
+        param_rows = NB * TILES
         rows_b_gamma = const.tile([P, P], BF16, name="rows_b_gamma")
         rows_beta = const.tile([P, P], BF16, name="rows_beta")
         nc.vector.memset(rows_beta[:], 0.0)
         eps_col = const.tile([P, 1], F32, name="eps_col")
         nc.vector.memset(eps_col[:], EPS)
-        param_rows = NB * TILES
         nc.scalar.dma_start(out=rows_b_gamma[:param_rows, :], in_=b.rearrange("k (i p) -> (k i) p", p=P))
         nc.scalar.dma_start(out=rows_b_gamma[param_rows:, :], in_=gamma.rearrange("k (i p) -> (k i) p", p=P))
         nc.scalar.dma_start(out=rows_beta[:param_rows, :], in_=beta.rearrange("k (i p) -> (k i) p", p=P))
@@ -249,29 +253,13 @@ def tile_extremeoptimizationlayer_pa_kernel(tc, x, W, b, gamma, beta, Wf1, bf1, 
         ident_bf16 = const.tile([P, P], BF16, name="ident_bf16")
         make_identity(nc, ident_bf16[:])
 
-        x_words = x_sb[:].bitcast(F32).rearrange("p (bt c q u) -> p bt c q u", bt=B // P, c=W_PASSES, q=P)
         x_grouped = const.tile([P, W_PASSES * B * PACK], BF16, name="x_grouped", align_bytes=64)
-        x_grouped_words = x_grouped[:].bitcast(F32).rearrange("p (c n u) -> p c n u", c=W_PASSES, n=B)
-        x_t = []
-        for c in range(W_PASSES):
-            x_t.append(psum_h.tile([P, 2, B], F32, name="h"))
-            for u in range(2):
-                for bt in range(B // P):
-                    nc.tensor.transpose(x_t[c][:, u, bt * P : (bt + 1) * P], x_words[:, bt, c, :, u], ident_f32[:])
-        params_t = psum_h.tile([P, 2, P], BF16, name="h")
-        nc.tensor.transpose(params_t[:, 0, :], rows_b_gamma[:], ident_bf16[:])
-        nc.tensor.transpose(params_t[:, 1, :], rows_beta[:], ident_bf16[:])
-        nc.vector.tensor_copy(out=x_grouped_words[:, 0], in_=x_t[0].rearrange("p u n -> p n u"))
-        nc.scalar.copy(out=x_grouped_words[:, 1], in_=x_t[1].rearrange("p u n -> p n u"))
+        x_codes = const.tile([P, W_PASSES * B], U32, name="x_codes", align_bytes=64)
+        x_scales = const.tile([P, W_PASSES * B], U8, name="x_scales", align_bytes=64)
         params = const.tile([P, 2, P], F32, name="params")
-        nc.vector.tensor_copy(out=params[:], in_=params_t[:])
         b_col = params[:, 0, :param_rows]
         gamma_col = params[:, 0, param_rows:]
         beta_col = params[:, 1, :param_rows]
-        x_codes = const.tile([P, W_PASSES * B], U32, name="x_codes", align_bytes=64)
-        x_scales = const.tile([P, W_PASSES * B], U8, name="x_scales", align_bytes=64)
-        nc.vector.quantize_mx(out=x_codes[:].bitcast(FP8X4), scales=x_scales[:], in_=x_grouped[:])
-
         f_codes = const.tile([P, F // K_PASS, B], U32, name="f_codes", align_bytes=64)
         f_scales = const.tile([P, F // K_PASS, B], U8, name="f_scales", align_bytes=64)
         acc = [
@@ -279,10 +267,32 @@ def tile_extremeoptimizationlayer_pa_kernel(tc, x, W, b, gamma, beta, Wf1, bf1, 
             for bt in range(B // P)
         ]
 
-        for r in range(ROUNDS + 1):
-            scalar_has_bn = live(r - 2)
-            vector_cols = VECTOR_COLS_BN if scalar_has_bn else VECTOR_COLS
+        def prepare_x_and_params():
+            x_words = x_sb[:].bitcast(F32).rearrange("p (bt c q u) -> p bt c q u", bt=B // P, c=W_PASSES, q=P)
+            x_grouped_words = x_grouped[:].bitcast(F32).rearrange("p (c n u) -> p c n u", c=W_PASSES, n=B)
+            x_t = []
+            for c in range(W_PASSES):
+                x_t.append(psum_h.tile([P, 2, B], F32, name="h"))
+                for u in range(2):
+                    for bt in range(B // P):
+                        nc.tensor.transpose(x_t[c][:, u, bt * P : (bt + 1) * P], x_words[:, bt, c, :, u], ident_f32[:])
+            params_t = psum_h.tile([P, 2, P], BF16, name="h")
+            nc.tensor.transpose(params_t[:, 0, :], rows_b_gamma[:], ident_bf16[:])
+            nc.tensor.transpose(params_t[:, 1, :], rows_beta[:], ident_bf16[:])
+            nc.vector.tensor_copy(out=x_grouped_words[:, 0], in_=x_t[0].rearrange("p u n -> p n u"))
+            nc.scalar.copy(out=x_grouped_words[:, 1], in_=x_t[1].rearrange("p u n -> p n u"))
+            nc.vector.tensor_copy(out=params[:], in_=params_t[:])
+            nc.vector.quantize_mx(out=x_codes[:].bitcast(FP8X4), scales=x_scales[:], in_=x_grouped[:])
+
+        def run_round(r):
             first = ROUND_SLABS * r
+            vector_cols = BASE_COLS
+            if live(r - 2):
+                vector_cols += RELU_SQUARES_COLS
+            if live(r - 3):
+                vector_cols -= NORMALISE_COLS
+            if live(r - 4):
+                vector_cols -= FUSED_COLS
 
             relu_and_sums(r - 2)
             standard_deviation(r - 3)
@@ -309,6 +319,11 @@ def tile_extremeoptimizationlayer_pa_kernel(tc, x, W, b, gamma, beta, Wf1, bf1, 
             shift(r - 3)
             normalise(r - 3)
             quantise_fused(r - 4)
+
+        run_round(0)
+        prepare_x_and_params()
+        for r in range(1, ROUNDS + 1):
+            run_round(r)
 
         for bt in range(B // P):
             for nt in range(DO // N_TILE):

@@ -30,8 +30,8 @@ N_TILE = 512
 RUN = 4
 
 RAW_BUFS = 10
-BASE_COLS = 512
-RELU_SQUARES_COLS = 416
+BASE_COLS = 448
+RELU_SQUARES_COLS = 480
 NORMALISE_COLS = 128
 FUSED_COLS = 128
 
@@ -39,7 +39,6 @@ FUSED_COLS = 128
 def tile_extremeoptimizationlayer_pa_kernel(tc, x, W, b, gamma, beta, Wf1, bf1, out):
     nc = tc.nc
     with ExitStack() as ctx:
-        ctx.enter_context(tc.manual_schedule())
         const = ctx.enter_context(tc.tile_pool(name="const", bufs=1))
         raw_pool = ctx.enter_context(tc.tile_pool(name="raw", bufs=RAW_BUFS))
         slab_pool = ctx.enter_context(tc.tile_pool(name="slab", bufs=2 * ROUND_SLABS))

from contextlib import ExitStack

import concourse.mybir as mybir
from concourse.masks import make_identity

F32 = mybir.dt.float32
BF16 = mybir.dt.bfloat16
U32 = mybir.dt.uint32
U8 = mybir.dt.uint8
FP8X4 = mybir.dt.float8_e4m3fn_x4
ACT = mybir.ActivationFunctionType
ALU = mybir.AluOpType

P = 128
PACK = 4
K_PASS = P * PACK
NB, DI, DO, B = 8, 1024, 1024, 256
F = NB * DO
EPS = 1e-5
FLOPS = 2 * B * DI * F + 2 * B * F * DO

TILES = DO // P
GROUPS = DO // K_PASS
W_PASSES = DI // K_PASS
W_SLABS = NB * W_PASSES
SLABS = W_SLABS + F // K_PASS
ROUND_SLABS = 2
ROUNDS = SLABS // ROUND_SLABS
N_TILE = 512
RUN = 4

RAW_BUFS = 10
BASE_COLS = 448
RELU_SQUARES_COLS = 480
NORMALISE_COLS = 128
FUSED_COLS = 128


def tile_extremeoptimizationlayer_pa_kernel(tc, x, W, b, gamma, beta, Wf1, bf1, out):
    nc = tc.nc
    with ExitStack() as ctx:
        const = ctx.enter_context(tc.tile_pool(name="const", bufs=1))
        raw_pool = ctx.enter_context(tc.tile_pool(name="raw", bufs=RAW_BUFS))
        slab_pool = ctx.enter_context(tc.tile_pool(name="slab", bufs=2 * ROUND_SLABS))
        branch_pool = ctx.enter_context(tc.tile_pool(name="branch", bufs=2))
        result_pool = ctx.enter_context(tc.tile_pool(name="result", bufs=4))
        psum_h = ctx.enter_context(tc.psum_pool(name="psum_h", bufs=4))
        psum_acc = ctx.enter_context(tc.psum_pool(name="psum_acc", bufs=1))

        raw_of = {}
        grouped_of = {}
        codes_of = {}
        h_of = {}
        bn = {}

        def load_slab(s):
            if s >= SLABS:
                return
            raw = raw_pool.tile([P, PACK, DO], BF16, name="raw")
            if s < W_SLABS:
                rows = W[s // W_PASSES, (s % W_PASSES) * K_PASS : (s % W_PASSES + 1) * K_PASS, :]
                nc.sync.dma_start(out=raw[:], in_=rows.rearrange("(p t) w -> p t w", t=PACK))
            else:
                g = s - W_SLABS
                rows = Wf1[g * K_PASS : (g + 1) * K_PASS, :]
                nc.sync.dma_start(out=raw[:], in_=rows.rearrange("(t p) w -> p t w", p=P))
            raw_of[s] = raw

        def regroup_slab(s, vector_cols):
            if s >= SLABS:
                return
            grouped = slab_pool.tile([P, DO, PACK], BF16, name="grouped", align_bytes=64)
            src = raw_of[s].rearrange("p t (c i) -> p c t i", i=RUN)
            dst = grouped.rearrange("p (c i) t -> p c t i", i=RUN)
            cut = vector_cols // RUN
            nc.vector.tensor_copy(out=dst[:, :cut], in_=src[:, :cut])
            nc.scalar.copy(out=dst[:, cut:], in_=src[:, cut:])
            grouped_of[s] = grouped

        def quantise_slab(s):
            if s < 0:
                return
            codes = slab_pool.tile([P, DO], U32, name="codes", align_bytes=64)
            scales = slab_pool.tile([P, DO], U8, name="scales", align_bytes=64)
            nc.vector.quantize_mx(
                out=codes[:].bitcast(FP8X4),
                scales=scales[:],
                in_=grouped_of[s].rearrange("p w t -> p (w t)"),
            )
            codes_of[s] = (codes, scales)

        def stage1(br):
            h_of[br] = []
            for pair in range(TILES // 2):
                h = psum_h.tile([P, 2, B], F32, name="h")
                for half in range(2):
                    cols = slice((2 * pair + half) * P, (2 * pair + half + 1) * P)
                    for c in range(W_PASSES):
                        codes, scales = codes_of[W_PASSES * br + c]
                        nc.tensor.matmul_mx(
                            out=h[:, half, :],
                            lhsT=codes[:, cols].bitcast(FP8X4),
                            lhsT_scale=scales[:, cols],
                            rhs=x_codes[:, c * B : (c + 1) * B].bitcast(FP8X4),
                            rhs_scale=x_scales[:, c * B : (c + 1) * B],
                            start=(c == 0),
                            stop=(c == W_PASSES - 1),
                        )
                h_of[br].append(h)

        def stage2(g):
            codes, scales = codes_of[W_SLABS + g]
            for bt in range(B // P):
                rows = slice(bt * P, (bt + 1) * P)
                for nt in range(DO // N_TILE):
                    cols = slice(nt * N_TILE, (nt + 1) * N_TILE)
                    nc.tensor.matmul_mx(
                        out=acc[bt][nt][:],
                        lhsT=f_codes[:, g, rows].bitcast(FP8X4),
                        lhsT_scale=f_scales[:, g, rows],
                        rhs=codes[:, cols].bitcast(FP8X4),
                        rhs_scale=scales[:, cols],
                        start=(g == 0),
                        stop=(g == F // K_PASS - 1),
                    )

        def live(br):
            return 0 <= br < NB

        def stat_tile(name, br):
            bn[(name, br)] = branch_pool.tile([P, TILES], F32, name=name)
            return bn[(name, br)]

        def relu_and_sums(br):
            if not live(br):
                return
            a = branch_pool.tile([P, TILES, B], F32, name="a")
            bn[("a", br)] = a
            sums = stat_tile("sums", br)
            for i in range(TILES):
                nc.scalar.activation(
                    out=a[:, i, :],
                    in_=h_of[br][i // 2][:, i % 2, :],
                    func=ACT.Relu,
                    bias=b_col[:, TILES * br + i : TILES * br + i + 1],
                    accum_out=sums[:, i : i + 1],
                )

        def negative_mean(br):
            if live(br):
                nc.scalar.mul(out=stat_tile("neg_mean", br)[:], in_=bn[("sums", br)][:], mul=-1.0 / B)

        def squares(br):
            if not live(br):
                return
            unused = branch_pool.tile([P, TILES, B], BF16, name="unused")
            sumsq = stat_tile("sumsq", br)
            for i in range(TILES):
                nc.scalar.activation(
                    out=unused[:, i, :],
                    in_=bn[("a", br)][:, i, :],
                    func=ACT.Square,
                    bias=bn[("neg_mean", br)][:, i : i + 1],
                    accum_out=sumsq[:, i : i + 1],
                )

        def standard_deviation(br):
            if live(br):
                nc.scalar.activation(
                    out=stat_tile("std", br)[:], in_=bn[("sumsq", br)][:], func=ACT.Sqrt, bias=eps_col[:], scale=1.0 / B
                )

        def reciprocal_std(br):
            if live(br):
                nc.vector.reciprocal(out=stat_tile("rstd", br)[:], in_=bn[("std", br)][:])

        def gain(br):
            if live(br):
                nc.vector.tensor_mul(
                    out=stat_tile("gain", br)[:], in0=bn[("rstd", br)][:], in1=gamma_col[:, TILES * br : TILES * (br + 1)]
                )

        def negative_mean_times_gain(br):
            if live(br):
                nc.vector.tensor_mul(out=stat_tile("moved", br)[:], in0=bn[("neg_mean", br)][:], in1=bn[("gain", br)][:])

        def shift(br):
            if live(br):
                nc.vector.tensor_add(
                    out=stat_tile("shift", br)[:], in0=bn[("moved", br)][:], in1=beta_col[:, TILES * br : TILES * (br + 1)]
                )

        def normalise(br):
            if not live(br):
                return
            normed = branch_pool.tile([P, TILES, B], BF16, name="normed")
            bn[("normed", br)] = normed
            for i in range(TILES):
                nc.vector.tensor_scalar(
                    out=normed[:, i, :],
                    in0=bn[("a", br)][:, i, :],
                    scalar1=bn[("gain", br)][:, i : i + 1],
                    scalar2=bn[("shift", br)][:, i : i + 1],
                    op0=ALU.mult,
                    op1=ALU.add,
                )

        def regroup_fused(br, j):
            if not live(br):
                return
            if j == 0:
                bn[("f_grouped", br)] = branch_pool.tile([P, GROUPS, B, PACK], BF16, name="f_grouped", align_bytes=64)
            nc.vector.tensor_copy(
                out=bn[("f_grouped", br)][:, j].rearrange("p (c i) t -> p c t i", i=RUN),
                in_=bn[("normed", br)][:, PACK * j : PACK * (j + 1), :].rearrange("p t (c i) -> p c t i", i=RUN),
            )

        def quantise_fused(br):
            if live(br):
                passes = slice(GROUPS * br, GROUPS * (br + 1))
                nc.vector.quantize_mx(
                    out=f_codes[:, passes, :].rearrange("p g n -> p (g n)").bitcast(FP8X4),
                    scales=f_scales[:, passes, :].rearrange("p g n -> p (g n)"),
                    in_=bn[("f_grouped", br)].rearrange("p g n t -> p (g n t)"),
                )

        x_sb = const.tile([P, (B // P) * DI], BF16, name="x_sb")
        for s in range(ROUND_SLABS):
            load_slab(s)
        nc.sync.dma_start(
            out=x_sb.rearrange("p (bt k) -> p bt k", k=DI), in_=x.rearrange("(bt p) k -> p bt k", p=P)
        )
        for s in range(ROUND_SLABS, RAW_BUFS):
            load_slab(s)
        bias_all = const.tile([P, DO], BF16, name="bias_all")
        nc.sync.dma_start(out=bias_all[:], in_=bf1.partition_broadcast(P))

        param_rows = NB * TILES
        rows_b_gamma = const.tile([P, P], BF16, name="rows_b_gamma")
        rows_beta = const.tile([P, P], BF16, name="rows_beta")
        nc.vector.memset(rows_beta[:], 0.0)
        eps_col = const.tile([P, 1], F32, name="eps_col")
        nc.vector.memset(eps_col[:], EPS)
        nc.scalar.dma_start(out=rows_b_gamma[:param_rows, :], in_=b.rearrange("k (i p) -> (k i) p", p=P))
        nc.scalar.dma_start(out=rows_b_gamma[param_rows:, :], in_=gamma.rearrange("k (i p) -> (k i) p", p=P))
        nc.scalar.dma_start(out=rows_beta[:param_rows, :], in_=beta.rearrange("k (i p) -> (k i) p", p=P))
        first_sqrt = const.tile([P, 1], F32, name="first_sqrt")
        nc.scalar.activation(out=first_sqrt[:], in_=eps_col[:], func=ACT.Sqrt)

        ident_f32 = const.tile([P, P], F32, name="ident_f32")
        make_identity(nc, ident_f32[:])
        ident_bf16 = const.tile([P, P], BF16, name="ident_bf16")
        make_identity(nc, ident_bf16[:])

        x_grouped = const.tile([P, W_PASSES * B * PACK], BF16, name="x_grouped", align_bytes=64)
        x_codes = const.tile([P, W_PASSES * B], U32, name="x_codes", align_bytes=64)
        x_scales = const.tile([P, W_PASSES * B], U8, name="x_scales", align_bytes=64)
        params = const.tile([P, 2, P], F32, name="params")
        b_col = params[:, 0, :param_rows]
        gamma_col = params[:, 0, param_rows:]
        beta_col = params[:, 1, :param_rows]
        f_codes = const.tile([P, F // K_PASS, B], U32, name="f_codes", align_bytes=64)
        f_scales = const.tile([P, F // K_PASS, B], U8, name="f_scales", align_bytes=64)
        acc = [
            [psum_acc.tile([P, N_TILE], F32, name="acc%d%d" % (bt, nt)) for nt in range(DO // N_TILE)]
            for bt in range(B // P)
        ]

        def prepare_x_and_params():
            x_words = x_sb[:].bitcast(F32).rearrange("p (bt c q u) -> p bt c q u", bt=B // P, c=W_PASSES, q=P)
            x_grouped_words = x_grouped[:].bitcast(F32).rearrange("p (c n u) -> p c n u", c=W_PASSES, n=B)
            x_t = []
            for c in range(W_PASSES):
                x_t.append(psum_h.tile([P, 2, B], F32, name="h"))
                for u in range(2):
                    for bt in range(B // P):
                        nc.tensor.transpose(x_t[c][:, u, bt * P : (bt + 1) * P], x_words[:, bt, c, :, u], ident_f32[:])
            params_t = psum_h.tile([P, 2, P], BF16, name="h")
            nc.tensor.transpose(params_t[:, 0, :], rows_b_gamma[:], ident_bf16[:])
            nc.tensor.transpose(params_t[:, 1, :], rows_beta[:], ident_bf16[:])
            nc.vector.tensor_copy(out=x_grouped_words[:, 0], in_=x_t[0].rearrange("p u n -> p n u"))
            nc.scalar.copy(out=x_grouped_words[:, 1], in_=x_t[1].rearrange("p u n -> p n u"))
            nc.vector.tensor_copy(out=params[:], in_=params_t[:])
            nc.vector.quantize_mx(out=x_codes[:].bitcast(FP8X4), scales=x_scales[:], in_=x_grouped[:])

        def run_round(r):
            first = ROUND_SLABS * r
            vector_cols = BASE_COLS
            if live(r - 2):
                vector_cols += RELU_SQUARES_COLS
            if live(r - 3):
                vector_cols -= NORMALISE_COLS
            if live(r - 4):
                vector_cols -= FUSED_COLS

            relu_and_sums(r - 2)
            standard_deviation(r - 3)
            quantise_slab(first - 2)
            quantise_slab(first - 1)
            if 1 <= r <= NB:
                stage1(r - 1)
            if r > NB:
                stage2(first - 2 - W_SLABS)
                stage2(first - 1 - W_SLABS)

            regroup_slab(first, vector_cols)
            reciprocal_std(r - 3)
            negative_mean(r - 2)
            regroup_slab(first + 1, vector_cols)
            load_slab(first + RAW_BUFS)
            load_slab(first + RAW_BUFS + 1)
            squares(r - 2)

            gain(r - 3)
            regroup_fused(r - 4, 0)
            negative_mean_times_gain(r - 3)
            regroup_fused(r - 4, 1)
            shift(r - 3)
            normalise(r - 3)
            quantise_fused(r - 4)

        run_round(0)
        prepare_x_and_params()
        for r in range(1, ROUNDS + 1):
            run_round(r)

        for bt in range(B // P):
            for nt in range(DO // N_TILE):
                cols = slice(nt * N_TILE, (nt + 1) * N_TILE)
                result = result_pool.tile([P, N_TILE], F32, name="result")
                nc.vector.tensor_tensor(out=result[:], in0=acc[bt][nt][:], in1=bias_all[:, cols], op=ALU.add)
                nc.scalar.activation(out=result[:], in_=result[:], func=ACT.Relu)
                nc.sync.dma_start(out=out[bt * P : (bt + 1) * P, cols], in_=result[:])
